import numpy as np
import ml_dtypes


def mxq(x, axis, fmt="e4m3"):
    dtype, down = {"e4m3": (ml_dtypes.float8_e4m3fn, 7), "e5m2": (ml_dtypes.float8_e5m2, 14)}[fmt]
    v = np.moveaxis(np.asarray(x, np.float32).astype(ml_dtypes.bfloat16).astype(np.float64), axis, -1)
    blocks = v.reshape(v.shape[:-1] + (-1, 32))
    amax = np.abs(blocks).max(-1, keepdims=True)
    byte = np.maximum(np.where(amax > 0, np.frexp(amax)[1] - 1 + 127, 0) - down, 1)
    scale = np.exp2(byte - 127.0)
    codes = (blocks / scale).astype(np.float32).astype(dtype).astype(np.float64)
    return np.moveaxis((codes * scale).reshape(v.shape), -1, axis)


WIDE = False


def mx_kscale(k):
    if not WIDE:
        return np.ones(k)
    levels = np.array([10, -10, 5, -5, 0])
    if k % 512:
        return np.exp2(np.random.permutation(np.resize(levels, k // 32))).repeat(32)
    a = np.empty((k // 512, 16))
    for p in range(k // 512):
        a[p, :8] = np.random.permutation(np.resize(levels, 8))
        for g in range(8):
            far = levels[np.abs(levels - a[p, g]) >= 10]
            a[p, g + 8] = far[np.random.randint(len(far))]
    return np.exp2(a.ravel()).repeat(32)


BF16 = ml_dtypes.bfloat16


def bf(x):
    return np.asarray(x, np.float32).astype(BF16)


def f64(x):
    return np.asarray(x).astype(np.float64)


B, S, D, H, F, QB = 4, 1024, 512, 4, 1536, 512
HD = D // H
EPS = 1e-5


def setup_inputs():
    s = mx_kscale(D)
    return {"x": bf(np.random.standard_normal((B, S, D))),
            "rms_w": bf((1.0 + 0.1 * np.random.standard_normal(D)) * s),
            "w_qkv": bf(np.random.standard_normal((3 * D, D)) * 1.5 / np.sqrt(D) / s[None, :])}


def reference(x, rms_w, w_qkv):
    xf = f64(x)
    xn = xf / np.sqrt(np.mean(xf * xf, axis=-1, keepdims=True) + EPS) * f64(rms_w)
    y = mxq(xn, 2, "e4m3") @ mxq(f64(w_qkv), 1, "e4m3").T
    return y.reshape(B, S, 3, H, HD).transpose(2, 0, 3, 1, 4)

@@ -1,0 +1,199 @@
+from contextlib import ExitStack
+
+import concourse.mybir as mybir
+from concourse.masks import make_identity
+
+F32 = mybir.dt.float32
+BF16 = mybir.dt.bfloat16
+U32 = mybir.dt.uint32
+U8 = mybir.dt.uint8
+FP8X4 = mybir.dt.float8_e4m3fn_x4
+ACT = mybir.ActivationFunctionType
+ALU = mybir.AluOpType
+
+P = 128
+PACK = 4
+B, S, D = 4, 1024, 512
+C, H, HD = 3, 4, 128
+EPS = 1e-5
+T = S // P
+N = H * HD
+PAIRS_PER_BATCH = T // 2
+
+FLOPS = 2 * B * S * C * N * D
+
+
+def tile_transformerblock_pa_t_kernel(tc, x, rms_w, w_qkv, out):
+    nc = tc.nc
+    with ExitStack() as stack:
+        keep = stack.enter_context(tc.tile_pool(name="keep", bufs=1))
+        squares = stack.enter_context(tc.tile_pool(name="squares", bufs=4))
+        scaled_pool = stack.enter_context(tc.tile_pool(name="scaled", bufs=8))
+        grouped_pool = stack.enter_context(tc.tile_pool(name="grouped", bufs=3))
+        w_grouped_pool = stack.enter_context(tc.tile_pool(name="w_grouped", bufs=2))
+        y_pool = stack.enter_context(tc.tile_pool(name="y", bufs=6))
+        flip_pool = stack.enter_context(tc.psum_pool(name="flip", bufs=4))
+        acc_pool = stack.enter_context(tc.psum_pool(name="acc", bufs=4))
+
+        ident = keep.tile([P, P], F32, name="ident")
+        eps = keep.tile([P, 1], F32, name="eps")
+        warm = keep.tile([P, 1], F32, name="warm")
+        gain = keep.tile([P, PACK], BF16, name="gain")
+        sumsq = keep.tile([P, B * T], F32, name="sumsq")
+        rinv = keep.tile([P, B * T], F32, name="rinv")
+        x_sb = [keep.tile([P, T * D], BF16, name="x%d" % b) for b in range(B)]
+        w_sb = [keep.tile([P, PACK * D], BF16, name="w%d" % c) for c in range(C)]
+        x_codes = keep.tile([P, B * T * P], U32, name="x_codes", align_bytes=64)
+        x_scales = keep.tile([P, B * T * P], U8, name="x_scales", align_bytes=64)
+        w_codes = keep.tile([P, C * N], U32, name="w_codes", align_bytes=64)
+        w_scales = keep.tile([P, C * N], U8, name="w_scales", align_bytes=64)
+        scaled = {}
+        flipped = {}
+        grouped = {}
+        y_tiles = {}
+
+        def load_x(b):
+            rows = x[b].rearrange("(p t) d -> p (t d)", t=T)
+            half = T * D // 2
+            for k in range(2):
+                nc.sync.dma_start(
+                    out=x_sb[b][:, k * half : (k + 1) * half], in_=rows[:, k * half : (k + 1) * half]
+                )
+
+        def load_w(c):
+            nc.sync.dma_start(
+                out=w_sb[c][:].rearrange("p (i k) -> p i k", k=D),
+                in_=w_qkv[c * N : (c + 1) * N, :].rearrange("(i p) k -> p i k", p=P),
+            )
+
+        def tile_of(g):
+            b, t = divmod(g, T)
+            return x_sb[b][:, t * D : (t + 1) * D]
+
+        def stats(q):
+            for g in (2 * q, 2 * q + 1):
+                sq = squares.tile([P, D], BF16, name="sq")
+                nc.scalar.activation(
+                    out=sq[:], in_=tile_of(g), func=ACT.Square, accum_out=sumsq[:, g : g + 1]
+                )
+            nc.scalar.activation(
+                out=rinv[:, 2 * q : 2 * q + 2],
+                in_=sumsq[:, 2 * q : 2 * q + 2],
+                func=ACT.Abs_reciprocal_sqrt,
+                bias=eps[:],
+                scale=1.0 / D,
+            )
+
+        def scale(q):
+            for g in (2 * q, 2 * q + 1):
+                scaled[g] = scaled_pool.tile([P, PACK, P], F32, name="scaled")
+                engine = nc.gpsimd if g % 2 == 0 else nc.vector
+                engine.tensor_scalar(
+                    out=scaled[g][:],
+                    in0=tile_of(g).rearrange("p (q t) -> p t q", t=PACK),
+                    scalar1=rinv[:, g : g + 1],
+                    scalar2=1.0,
+                    op0=ALU.mult,
+                    op1=ALU.mult,
+                )
+
+        def flip(q):
+            for g in (2 * q, 2 * q + 1):
+                flipped[g] = flip_pool.tile([P, PACK, P], F32, name="flipped")
+                for t in range(PACK):
+                    nc.tensor.transpose(flipped[g][:, t, :], scaled[g][:, t, :], ident[:])
+
+        def pack(q):
+            grouped[q] = grouped_pool.tile([P, 2 * P * PACK], BF16, name="grouped", align_bytes=64)
+            for k in range(2):
+                nc.vector.tensor_tensor(
+                    out=grouped[q][:, k * P * PACK : (k + 1) * P * PACK].rearrange(
+                        "p (r t) -> p r t", t=PACK
+                    ),
+                    in0=flipped[2 * q + k][:].rearrange("p t r -> p r t"),
+                    in1=gain[:].unsqueeze(1).to_broadcast([P, P, PACK]),
+                    op=ALU.mult,
+                )
+
+        def quantise(q):
+            cols = slice(2 * q * P, (2 * q + 2) * P)
+            nc.vector.quantize_mx(
+                out=x_codes[:, cols].bitcast(FP8X4), scales=x_scales[:, cols], in_=grouped[q][:]
+            )
+
+        def weights(c):
+            w_words = w_sb[c][:].bitcast(F32)
+            w_grouped = w_grouped_pool.tile([P, N * PACK], BF16, name="w_grouped", align_bytes=64)
+            g_words = w_grouped[:].bitcast(F32)
+            for k in range(2):
+                w_flipped = flip_pool.tile([P, PACK, P], F32, name="flipped")
+                for s in range(PACK):
+                    i, u = divmod(k * PACK + s, 2)
+                    pairs = w_words[:, i * D // 2 + u : (i + 1) * D // 2 : 2]
+                    nc.tensor.transpose(w_flipped[:, s, :], pairs, ident[:])
+                dst = g_words[:, k * N : (k + 1) * N].rearrange("p (i f u) -> p i f u", i=2, u=2)
+                src = w_flipped[:].rearrange("p (i u) f -> p i f u", u=2)
+                if k == 0:
+                    nc.vector.tensor_copy(out=dst, in_=src)
+                else:
+                    nc.scalar.copy(out=dst, in_=src)
+            cols = slice(c * N, (c + 1) * N)
+            nc.vector.quantize_mx(
+                out=w_codes[:, cols].bitcast(FP8X4), scales=w_scales[:, cols], in_=w_grouped[:]
+            )
+
+        def project(n):
+            b, rest = divmod(n, C * T)
+            c, t = divmod(rest, T)
+            tok = slice((b * T + t) * P, (b * T + t + 1) * P)
+            feat = slice(c * N, (c + 1) * N)
+            acc = acc_pool.tile([P, N], F32, name="acc")
+            nc.tensor.matmul_mx(
+                out=acc[:],
+                lhsT=x_codes[:, tok].bitcast(FP8X4),
+                lhsT_scale=x_scales[:, tok],
+                rhs=w_codes[:, feat].bitcast(FP8X4),
+                rhs_scale=w_scales[:, feat],
+                start=True,
+                stop=True,
+            )
+            if t == 0:
+                y_tiles[(b, c)] = y_pool.tile([P, H, T, HD], F32, name="y")
+            y = y_tiles[(b, c)]
+            src = acc[:].rearrange("p (h j) -> p h j", h=H)
+            if n % 3 != 2:
+                nc.scalar.copy(out=y[:, :, t, :], in_=src)
+            else:
+                nc.vector.tensor_copy(out=y[:, :, t, :], in_=src)
+            if t == T - 1:
+                nc.sync.dma_start(
+                    out=out[c, b].rearrange("h (p t) j -> p h (t j)", t=T),
+                    in_=y[:].rearrange("p h t j -> p h (t j)"),
+                )
+
+        nc.vector.memset(eps[:], EPS)
+        nc.scalar.activation(out=warm[:], in_=eps[:], func=ACT.Abs_reciprocal_sqrt)
+        make_identity(nc, ident[:])
+        nc.scalar.dma_start(out=gain[:], in_=rms_w.rearrange("(q t) -> q t", t=PACK))
+        load_x(0)
+        for c in range(C):
+            load_w(c)
+        for b in range(1, B):
+            load_x(b)
+
+        weights(0)
+        for b in range(B):
+            for j in range(PAIRS_PER_BATCH):
+                q = b * PAIRS_PER_BATCH + j
+                stats(q)
+                scale(q)
+                flip(q)
+                pack(q)
+                quantise(q)
+                project(b * C * T + 2 * j)
+                project(b * C * T + 2 * j + 1)
+            for c in range(1, C):
+                if b == 0:
+                    weights(c)
+                for t in range(T):
+                    project((b * C + c) * T + t)

@@ -18,7 +18,7 @@ C, H, HD = 3, 4, 128
 EPS = 1e-5
 T = S // P
 N = H * HD
-PAIRS_PER_BATCH = T // 2
+GROUPS = [(0, 0, T // 2), (0, T // 2, T // 2)] + [(b, 0, T) for b in range(1, B)]
 
 FLOPS = 2 * B * S * C * N * D
 
@@ -52,13 +52,13 @@ def tile_transformerblock_pa_t_kernel(tc, x, rms_w, w_qkv, out):
         grouped = {}
         y_tiles = {}
 
-        def load_x(b):
-            rows = x[b].rearrange("(p t) d -> p (t d)", t=T)
-            half = T * D // 2
-            for k in range(2):
-                nc.sync.dma_start(
-                    out=x_sb[b][:, k * half : (k + 1) * half], in_=rows[:, k * half : (k + 1) * half]
-                )
+        def load_x(group, parts):
+            b, first, size = group
+            rows = x[b, first * P : (first + size) * P, :].rearrange("(p t) d -> p (t d)", t=size)
+            width = size * D // parts
+            for k in range(parts):
+                cols = slice(first * D + k * width, first * D + (k + 1) * width)
+                nc.sync.dma_start(out=x_sb[b][:, cols], in_=rows[:, k * width : (k + 1) * width])
 
         def load_w(c):
             nc.sync.dma_start(
@@ -142,10 +142,10 @@ def tile_transformerblock_pa_t_kernel(tc, x, rms_w, w_qkv, out):
                 out=w_codes[:, cols].bitcast(FP8X4), scales=w_scales[:, cols], in_=w_grouped[:]
             )
 
-        def project(n):
-            b, rest = divmod(n, C * T)
-            c, t = divmod(rest, T)
-            tok = slice((b * T + t) * P, (b * T + t + 1) * P)
+        def project(n, group, c, g):
+            b, first, size = group
+            t = g - b * T - first
+            tok = slice(g * P, (g + 1) * P)
             feat = slice(c * N, (c + 1) * N)
             acc = acc_pool.tile([P, N], F32, name="acc")
             nc.tensor.matmul_mx(
@@ -158,16 +158,17 @@ def tile_transformerblock_pa_t_kernel(tc, x, rms_w, w_qkv, out):
                 stop=True,
             )
             if t == 0:
-                y_tiles[(b, c)] = y_pool.tile([P, H, T, HD], F32, name="y")
-            y = y_tiles[(b, c)]
+                y_tiles[c] = y_pool.tile([P, H, size, HD], F32, name="y")
+            y = y_tiles[c]
             src = acc[:].rearrange("p (h j) -> p h j", h=H)
-            if n % 3 != 2:
+            if n % 7 % 2 == 0:
                 nc.scalar.copy(out=y[:, :, t, :], in_=src)
             else:
                 nc.vector.tensor_copy(out=y[:, :, t, :], in_=src)
-            if t == T - 1:
+            if t == size - 1:
+                rows = out[c, b][:, first * P : (first + size) * P, :]
                 nc.sync.dma_start(
-                    out=out[c, b].rearrange("h (p t) j -> p h (t j)", t=T),
+                    out=rows.rearrange("h (p t) j -> p h (t j)", t=size),
                     in_=y[:].rearrange("p h t j -> p h (t j)"),
                 )
 
@@ -175,25 +176,26 @@ def tile_transformerblock_pa_t_kernel(tc, x, rms_w, w_qkv, out):
         nc.scalar.activation(out=warm[:], in_=eps[:], func=ACT.Abs_reciprocal_sqrt)
         make_identity(nc, ident[:])
         nc.scalar.dma_start(out=gain[:], in_=rms_w.rearrange("(q t) -> q t", t=PACK))
-        load_x(0)
-        for c in range(C):
-            load_w(c)
-        for b in range(1, B):
-            load_x(b)
+        load_x(GROUPS[0], 2)
+        load_w(0)
+        load_w(1)
+        load_w(2)
+        for group in GROUPS[1:]:
+            load_x(group, 1)
 
-        weights(0)
-        for b in range(B):
-            for j in range(PAIRS_PER_BATCH):
-                q = b * PAIRS_PER_BATCH + j
+        n = 0
+        for group in GROUPS:
+            b, first, size = group
+            for j in range(size // 2):
+                q = (b * T + first) // 2 + j
                 stats(q)
                 scale(q)
                 flip(q)
                 pack(q)
                 quantise(q)
-                project(b * C * T + 2 * j)
-                project(b * C * T + 2 * j + 1)
-            for c in range(1, C):
-                if b == 0:
-                    weights(c)
-                for t in range(T):
-                    project((b * C + c) * T + t)
+                for c in range(C):
+                    if q == 0:
+                        weights(c)
+                    for g in (2 * q, 2 * q + 1):
+                        project(n, group, c, g)
+                        n += 1

@@ -16,9 +16,10 @@ PACK = 4
 B, S, D = 4, 1024, 512
 C, H, HD = 3, 4, 128
 EPS = 1e-5
-T = S // P
 N = H * HD
-GROUPS = [(0, 0, T // 2), (0, T // 2, T // 2)] + [(b, 0, T) for b in range(1, B)]
+G = 4
+GROUPS = B * S // (G * P)
+GROUPS_PER_BATCH = GROUPS // B
 
 FLOPS = 2 * B * S * C * N * D
 
@@ -27,38 +28,42 @@ def tile_transformerblock_pa_t_kernel(tc, x, rms_w, w_qkv, out):
     nc = tc.nc
     with ExitStack() as stack:
         keep = stack.enter_context(tc.tile_pool(name="keep", bufs=1))
-        squares = stack.enter_context(tc.tile_pool(name="squares", bufs=4))
-        scaled_pool = stack.enter_context(tc.tile_pool(name="scaled", bufs=8))
-        grouped_pool = stack.enter_context(tc.tile_pool(name="grouped", bufs=3))
+        squares = stack.enter_context(tc.tile_pool(name="squares", bufs=2))
+        scaled_pool = stack.enter_context(tc.tile_pool(name="scaled", bufs=2 * G + 2))
+        grouped_pool = stack.enter_context(tc.tile_pool(name="grouped", bufs=4))
         w_grouped_pool = stack.enter_context(tc.tile_pool(name="w_grouped", bufs=2))
-        y_pool = stack.enter_context(tc.tile_pool(name="y", bufs=6))
-        flip_pool = stack.enter_context(tc.psum_pool(name="flip", bufs=4))
-        acc_pool = stack.enter_context(tc.psum_pool(name="acc", bufs=4))
+        y_pool = stack.enter_context(tc.tile_pool(name="y", bufs=12))
+        flip_pool = stack.enter_context(tc.psum_pool(name="flip", bufs=2))
+        acc_pool = stack.enter_context(tc.psum_pool(name="acc", bufs=6))
 
         ident = keep.tile([P, P], F32, name="ident")
         eps = keep.tile([P, 1], F32, name="eps")
         warm = keep.tile([P, 1], F32, name="warm")
         gain = keep.tile([P, PACK], BF16, name="gain")
-        sumsq = keep.tile([P, B * T], F32, name="sumsq")
-        rinv = keep.tile([P, B * T], F32, name="rinv")
-        x_sb = [keep.tile([P, T * D], BF16, name="x%d" % b) for b in range(B)]
+        sumsq = keep.tile([P, GROUPS * G], F32, name="sumsq")
+        rinv = keep.tile([P, GROUPS * G], F32, name="rinv")
+        x_sb = [keep.tile([P, G * D], BF16, name="x%d" % k) for k in range(GROUPS)]
         w_sb = [keep.tile([P, PACK * D], BF16, name="w%d" % c) for c in range(C)]
-        x_codes = keep.tile([P, B * T * P], U32, name="x_codes", align_bytes=64)
-        x_scales = keep.tile([P, B * T * P], U8, name="x_scales", align_bytes=64)
+        x_codes = keep.tile([P, GROUPS * G * P], U32, name="x_codes", align_bytes=64)
+        x_scales = keep.tile([P, GROUPS * G * P], U8, name="x_scales", align_bytes=64)
         w_codes = keep.tile([P, C * N], U32, name="w_codes", align_bytes=64)
         w_scales = keep.tile([P, C * N], U8, name="w_scales", align_bytes=64)
         scaled = {}
         flipped = {}
         grouped = {}
+        w_flipped = {}
+        w_grouped = {}
         y_tiles = {}
 
-        def load_x(group, parts):
-            b, first, size = group
-            rows = x[b, first * P : (first + size) * P, :].rearrange("(p t) d -> p (t d)", t=size)
-            width = size * D // parts
-            for k in range(parts):
-                cols = slice(first * D + k * width, first * D + (k + 1) * width)
-                nc.sync.dma_start(out=x_sb[b][:, cols], in_=rows[:, k * width : (k + 1) * width])
+        def rows_of(k):
+            return slice(k % GROUPS_PER_BATCH * G * P, (k % GROUPS_PER_BATCH + 1) * G * P)
+
+        def load_x(k, parts):
+            rows = x[k // GROUPS_PER_BATCH, rows_of(k), :].rearrange("(p t) d -> p (t d)", t=G)
+            width = G * D // parts
+            for i in range(parts):
+                cols = slice(i * width, (i + 1) * width)
+                nc.sync.dma_start(out=x_sb[k][:, cols], in_=rows[:, cols])
 
         def load_w(c):
             nc.sync.dma_start(
@@ -67,89 +72,94 @@ def tile_transformerblock_pa_t_kernel(tc, x, rms_w, w_qkv, out):
             )
 
         def tile_of(g):
-            b, t = divmod(g, T)
-            return x_sb[b][:, t * D : (t + 1) * D]
+            return x_sb[g // G][:, g % G * D : (g % G + 1) * D]
 
-        def stats(q):
-            for g in (2 * q, 2 * q + 1):
-                sq = squares.tile([P, D], BF16, name="sq")
-                nc.scalar.activation(
-                    out=sq[:], in_=tile_of(g), func=ACT.Square, accum_out=sumsq[:, g : g + 1]
-                )
+        def square_sum(g):
+            sq = squares.tile([P, D], BF16, name="sq")
             nc.scalar.activation(
-                out=rinv[:, 2 * q : 2 * q + 2],
-                in_=sumsq[:, 2 * q : 2 * q + 2],
+                out=sq[:], in_=tile_of(g), func=ACT.Square, accum_out=sumsq[:, g : g + 1]
+            )
+
+        def inverse_rms(g):
+            nc.scalar.activation(
+                out=rinv[:, g : g + 2],
+                in_=sumsq[:, g : g + 2],
                 func=ACT.Abs_reciprocal_sqrt,
                 bias=eps[:],
                 scale=1.0 / D,
             )
 
-        def scale(q):
-            for g in (2 * q, 2 * q + 1):
-                scaled[g] = scaled_pool.tile([P, PACK, P], F32, name="scaled")
-                engine = nc.gpsimd if g % 2 == 0 else nc.vector
-                engine.tensor_scalar(
-                    out=scaled[g][:],
-                    in0=tile_of(g).rearrange("p (q t) -> p t q", t=PACK),
-                    scalar1=rinv[:, g : g + 1],
-                    scalar2=1.0,
-                    op0=ALU.mult,
-                    op1=ALU.mult,
-                )
-
-        def flip(q):
-            for g in (2 * q, 2 * q + 1):
-                flipped[g] = flip_pool.tile([P, PACK, P], F32, name="flipped")
-                for t in range(PACK):
-                    nc.tensor.transpose(flipped[g][:, t, :], scaled[g][:, t, :], ident[:])
-
-        def pack(q):
-            grouped[q] = grouped_pool.tile([P, 2 * P * PACK], BF16, name="grouped", align_bytes=64)
-            for k in range(2):
-                nc.vector.tensor_tensor(
-                    out=grouped[q][:, k * P * PACK : (k + 1) * P * PACK].rearrange(
-                        "p (r t) -> p r t", t=PACK
-                    ),
-                    in0=flipped[2 * q + k][:].rearrange("p t r -> p r t"),
-                    in1=gain[:].unsqueeze(1).to_broadcast([P, P, PACK]),
-                    op=ALU.mult,
-                )
-
-        def quantise(q):
-            cols = slice(2 * q * P, (2 * q + 2) * P)
-            nc.vector.quantize_mx(
-                out=x_codes[:, cols].bitcast(FP8X4), scales=x_scales[:, cols], in_=grouped[q][:]
+        def scale(engine, g):
+            scaled[g] = scaled_pool.tile([P, PACK, P], F32, name="scaled")
+            engine.tensor_scalar(
+                out=scaled[g][:],
+                in0=tile_of(g).rearrange("p (q t) -> p t q", t=PACK),
+                scalar1=rinv[:, g : g + 1],
+                scalar2=1.0,
+                op0=ALU.mult,
+                op1=ALU.mult,
             )
 
-        def weights(c):
+        def flip(g):
+            flipped[g] = flip_pool.tile([P, PACK, P], F32, name="flipped")
+            for t in range(PACK):
+                nc.tensor.transpose(flipped[g][:, t, :], scaled[g][:, t, :], ident[:])
+
+        def pack(g):
+            if g % 2 == 0:
+                grouped[g // 2] = grouped_pool.tile(
+                    [P, 2 * P * PACK], BF16, name="grouped", align_bytes=64
+                )
+            k = g % 2
+            nc.vector.tensor_tensor(
+                out=grouped[g // 2][:, k * P * PACK : (k + 1) * P * PACK].rearrange(
+                    "p (r t) -> p r t", t=PACK
+                ),
+                in0=flipped[g][:].rearrange("p t r -> p r t"),
+                in1=gain[:].unsqueeze(1).to_broadcast([P, P, PACK]),
+                op=ALU.mult,
+            )
+
+        def quantise(g):
+            cols = slice(g * P, (g + 2) * P)
+            nc.vector.quantize_mx(
+                out=x_codes[:, cols].bitcast(FP8X4),
+                scales=x_scales[:, cols],
+                in_=grouped[g // 2][:],
+            )
+
+        def flip_w(c):
             w_words = w_sb[c][:].bitcast(F32)
-            w_grouped = w_grouped_pool.tile([P, N * PACK], BF16, name="w_grouped", align_bytes=64)
-            g_words = w_grouped[:].bitcast(F32)
             for k in range(2):
-                w_flipped = flip_pool.tile([P, PACK, P], F32, name="flipped")
+                w_flipped[(c, k)] = acc_pool.tile([P, PACK, P], F32, name="acc")
                 for s in range(PACK):
                     i, u = divmod(k * PACK + s, 2)
-                    pairs = w_words[:, i * D // 2 + u : (i + 1) * D // 2 : 2]
-                    nc.tensor.transpose(w_flipped[:, s, :], pairs, ident[:])
-                dst = g_words[:, k * N : (k + 1) * N].rearrange("p (i f u) -> p i f u", i=2, u=2)
-                src = w_flipped[:].rearrange("p (i u) f -> p i f u", u=2)
-                if k == 0:
-                    nc.vector.tensor_copy(out=dst, in_=src)
-                else:
-                    nc.scalar.copy(out=dst, in_=src)
-            cols = slice(c * N, (c + 1) * N)
-            nc.vector.quantize_mx(
-                out=w_codes[:, cols].bitcast(FP8X4), scales=w_scales[:, cols], in_=w_grouped[:]
+                    words = w_words[:, i * D // 2 + u : (i + 1) * D // 2 : 2]
+                    nc.tensor.transpose(w_flipped[(c, k)][:, s, :], words, ident[:])
+
+        def copy_w(copy, c, k):
+            if k == 0:
+                w_grouped[c] = w_grouped_pool.tile(
+                    [P, N * PACK], BF16, name="w_grouped", align_bytes=64
+                )
+            words = w_grouped[c][:].bitcast(F32)[:, k * N : (k + 1) * N]
+            copy(
+                out=words.rearrange("p (i f u) -> p i f u", i=2, u=2),
+                in_=w_flipped[(c, k)][:].rearrange("p (i u) f -> p i f u", u=2),
             )
 
-        def project(n, group, c, g):
-            b, first, size = group
-            t = g - b * T - first
-            tok = slice(g * P, (g + 1) * P)
+        def quantise_w(c):
+            cols = slice(c * N, (c + 1) * N)
+            nc.vector.quantize_mx(
+                out=w_codes[:, cols].bitcast(FP8X4), scales=w_scales[:, cols], in_=w_grouped[c][:]
+            )
+
+        def project(copy, k, c, t):
+            tok = slice((k * G + t) * P, (k * G + t + 1) * P)
             feat = slice(c * N, (c + 1) * N)
-            acc = acc_pool.tile([P, N], F32, name="acc")
+            acc = acc_pool.tile([P, H, HD], F32, name="acc")
             nc.tensor.matmul_mx(
-                out=acc[:],
+                out=acc[:].rearrange("p h j -> p (h j)"),
                 lhsT=x_codes[:, tok].bitcast(FP8X4),
                 lhsT_scale=x_scales[:, tok],
                 rhs=w_codes[:, feat].bitcast(FP8X4),
@@ -158,44 +168,115 @@ def tile_transformerblock_pa_t_kernel(tc, x, rms_w, w_qkv, out):
                 stop=True,
             )
             if t == 0:
-                y_tiles[c] = y_pool.tile([P, H, size, HD], F32, name="y")
-            y = y_tiles[c]
-            src = acc[:].rearrange("p (h j) -> p h j", h=H)
-            if n % 7 % 2 == 0:
-                nc.scalar.copy(out=y[:, :, t, :], in_=src)
-            else:
-                nc.vector.tensor_copy(out=y[:, :, t, :], in_=src)
-            if t == size - 1:
-                rows = out[c, b][:, first * P : (first + size) * P, :]
-                nc.sync.dma_start(
-                    out=rows.rearrange("h (p t) j -> p h (t j)", t=size),
-                    in_=y[:].rearrange("p h t j -> p h (t j)"),
-                )
+                y_tiles[c] = y_pool.tile([P, H, G, HD], F32, name="y")
+            copy(out=y_tiles[c][:, :, t, :], in_=acc[:])
+
+        def store(k, c):
+            nc.sync.dma_start(
+                out=out[c, k // GROUPS_PER_BATCH][:, rows_of(k), :].rearrange(
+                    "h (p t) j -> p h (t j)", t=G
+                ),
+                in_=y_tiles[c][:].rearrange("p h t j -> p h (t j)"),
+            )
+
+        def measure(g):
+            square_sum(g)
+            square_sum(g + 1)
+            inverse_rms(g)
+
+        def flip_two(g):
+            flip(g)
+            flip(g + 1)
+
+        scalar_copy, vector_copy = nc.scalar.copy, nc.vector.tensor_copy
 
         nc.vector.memset(eps[:], EPS)
         nc.scalar.activation(out=warm[:], in_=eps[:], func=ACT.Abs_reciprocal_sqrt)
         make_identity(nc, ident[:])
         nc.scalar.dma_start(out=gain[:], in_=rms_w.rearrange("(q t) -> q t", t=PACK))
-        load_x(GROUPS[0], 2)
+        stack.enter_context(tc.manual_schedule())
+        load_x(0, 2)
         load_w(0)
+        load_x(1, 1)
         load_w(1)
         load_w(2)
-        for group in GROUPS[1:]:
-            load_x(group, 1)
+        for k in range(2, GROUPS):
+            load_x(k, 1)
 
-        n = 0
-        for group in GROUPS:
-            b, first, size = group
-            for j in range(size // 2):
-                q = (b * T + first) // 2 + j
-                stats(q)
-                scale(q)
-                flip(q)
-                pack(q)
-                quantise(q)
-                for c in range(C):
-                    if q == 0:
-                        weights(c)
-                    for g in (2 * q, 2 * q + 1):
-                        project(n, group, c, g)
-                        n += 1
+        measure(0)
+        scale(nc.vector, 0)
+        scale(nc.vector, 1)
+        flip_w(0)
+        copy_w(vector_copy, 0, 0)
+        flip_two(0)
+        measure(2)
+        copy_w(scalar_copy, 0, 1)
+        scale(nc.vector, 2)
+        scale(nc.vector, 3)
+        pack(0)
+        pack(1)
+        quantise_w(0)
+        quantise(0)
+        measure(G)
+        scale(nc.gpsimd, G)
+        scale(nc.gpsimd, G + 1)
+        flip_two(2)
+        pack(2)
+        pack(3)
+        flip_w(1)
+        copy_w(vector_copy, 1, 0)
+        copy_w(scalar_copy, 1, 1)
+        quantise(2)
+        for t in range(G):
+            project(scalar_copy if t % 2 == 0 else vector_copy, 0, 0, t)
+        store(0, 0)
+        quantise_w(1)
+        flip_w(2)
+        copy_w(vector_copy, 2, 0)
+        copy_w(scalar_copy, 2, 1)
+        for t in range(G):
+            project(scalar_copy if t % 2 == 0 else vector_copy, 0, 1, t)
+        store(0, 1)
+        quantise_w(2)
+        measure(G + 2)
+        scale(nc.gpsimd, G + 2)
+        scale(nc.gpsimd, G + 3)
+        flip_two(G)
+        pack(G)
+        pack(G + 1)
+        for t in range(G):
+            project(scalar_copy if t % 2 == 0 else vector_copy, 0, 2, t)
+        store(0, 2)
+        quantise(G)
+        measure(2 * G)
+        scale(nc.gpsimd, 2 * G)
+        scale(nc.gpsimd, 2 * G + 1)
+        flip_two(G + 2)
+        pack(G + 2)
+        pack(G + 3)
+        quantise(G + 2)
+
+        for i in range(2, 2 * GROUPS):
+            packed = 2 * (i + 2) if i + 2 < 2 * GROUPS else None
+            measured = 2 * (i + 3) if i + 3 < 2 * GROUPS else None
+            for m in range(6):
+                c, t = divmod(i % 2 * 6 + m, G)
+                if measured is not None:
+                    if m == 0:
+                        square_sum(measured)
+                        square_sum(measured + 1)
+                    if m == 2:
+                        inverse_rms(measured)
+                        scale(nc.gpsimd, measured)
+                        scale(nc.gpsimd, measured + 1)
+                if packed is not None:
+                    if m == 4:
+                        flip_two(packed)
+                        pack(packed)
+                    if m == 5:
+                        pack(packed + 1)
+                project(scalar_copy if m % 2 == 0 else vector_copy, i // 2, c, t)
+                if t == G - 1:
+                    store(i // 2, c)
+            if packed is not None:
+                quantise(packed)

@@ -17,9 +17,10 @@ B, S, D = 4, 1024, 512
 C, H, HD = 3, 4, 128
 EPS = 1e-5
 N = H * HD
-G = 4
-GROUPS = B * S // (G * P)
-GROUPS_PER_BATCH = GROUPS // B
+T = S // P
+PAIRS = B * T // 2
+GROUPS = [(b, i, i + 4) for b in range(B) for i in (0, 4)]
+PRODUCTS = [(b, i, j, c, t) for b, i, j in GROUPS for c in range(C) for t in range(i, j)]
 
 FLOPS = 2 * B * S * C * N * D
 
@@ -29,10 +30,10 @@ def tile_transformerblock_pa_t_kernel(tc, x, rms_w, w_qkv, out):
     with ExitStack() as stack:
         keep = stack.enter_context(tc.tile_pool(name="keep", bufs=1))
         squares = stack.enter_context(tc.tile_pool(name="squares", bufs=2))
-        scaled_pool = stack.enter_context(tc.tile_pool(name="scaled", bufs=2 * G + 2))
+        scaled_pool = stack.enter_context(tc.tile_pool(name="scaled", bufs=8))
         grouped_pool = stack.enter_context(tc.tile_pool(name="grouped", bufs=4))
         w_grouped_pool = stack.enter_context(tc.tile_pool(name="w_grouped", bufs=2))
-        y_pool = stack.enter_context(tc.tile_pool(name="y", bufs=12))
+        y_pool = stack.enter_context(tc.tile_pool(name="y", bufs=7))
         flip_pool = stack.enter_context(tc.psum_pool(name="flip", bufs=2))
         acc_pool = stack.enter_context(tc.psum_pool(name="acc", bufs=6))
 
@@ -40,12 +41,12 @@ def tile_transformerblock_pa_t_kernel(tc, x, rms_w, w_qkv, out):
         eps = keep.tile([P, 1], F32, name="eps")
         warm = keep.tile([P, 1], F32, name="warm")
         gain = keep.tile([P, PACK], BF16, name="gain")
-        sumsq = keep.tile([P, GROUPS * G], F32, name="sumsq")
-        rinv = keep.tile([P, GROUPS * G], F32, name="rinv")
-        x_sb = [keep.tile([P, G * D], BF16, name="x%d" % k) for k in range(GROUPS)]
+        sumsq = keep.tile([P, B * T], F32, name="sumsq")
+        rinv = keep.tile([P, B * T], F32, name="rinv")
+        x_sb = [keep.tile([P, T * D], BF16, name="x%d" % b) for b in range(B)]
         w_sb = [keep.tile([P, PACK * D], BF16, name="w%d" % c) for c in range(C)]
-        x_codes = keep.tile([P, GROUPS * G * P], U32, name="x_codes", align_bytes=64)
-        x_scales = keep.tile([P, GROUPS * G * P], U8, name="x_scales", align_bytes=64)
+        x_codes = keep.tile([P, B * T * P], U32, name="x_codes", align_bytes=64)
+        x_scales = keep.tile([P, B * T * P], U8, name="x_scales", align_bytes=64)
         w_codes = keep.tile([P, C * N], U32, name="w_codes", align_bytes=64)
         w_scales = keep.tile([P, C * N], U8, name="w_scales", align_bytes=64)
         scaled = {}
@@ -55,15 +56,10 @@ def tile_transformerblock_pa_t_kernel(tc, x, rms_w, w_qkv, out):
         w_grouped = {}
         y_tiles = {}
 
-        def rows_of(k):
-            return slice(k % GROUPS_PER_BATCH * G * P, (k % GROUPS_PER_BATCH + 1) * G * P)
-
-        def load_x(k, parts):
-            rows = x[k // GROUPS_PER_BATCH, rows_of(k), :].rearrange("(p t) d -> p (t d)", t=G)
-            width = G * D // parts
-            for i in range(parts):
-                cols = slice(i * width, (i + 1) * width)
-                nc.sync.dma_start(out=x_sb[k][:, cols], in_=rows[:, cols])
+        def load_x(b, first, last):
+            cols = slice(first * D, last * D)
+            rows = x[b].rearrange("(p t) d -> p (t d)", t=T)
+            nc.sync.dma_start(out=x_sb[b][:, cols], in_=rows[:, cols])
 
         def load_w(c):
             nc.sync.dma_start(
@@ -72,7 +68,8 @@ def tile_transformerblock_pa_t_kernel(tc, x, rms_w, w_qkv, out):
             )
 
         def tile_of(g):
-            return x_sb[g // G][:, g % G * D : (g % G + 1) * D]
+            b, t = divmod(g, T)
+            return x_sb[b][:, t * D : (t + 1) * D]
 
         def square_sum(g):
             sq = squares.tile([P, D], BF16, name="sq")
@@ -154,8 +151,9 @@ def tile_transformerblock_pa_t_kernel(tc, x, rms_w, w_qkv, out):
                 out=w_codes[:, cols].bitcast(FP8X4), scales=w_scales[:, cols], in_=w_grouped[c][:]
             )
 
-        def project(copy, k, c, t):
-            tok = slice((k * G + t) * P, (k * G + t + 1) * P)
+        def project(copy, n):
+            b, first, last, c, t = PRODUCTS[n]
+            tok = slice((b * T + t) * P, (b * T + t + 1) * P)
             feat = slice(c * N, (c + 1) * N)
             acc = acc_pool.tile([P, H, HD], F32, name="acc")
             nc.tensor.matmul_mx(
@@ -167,17 +165,15 @@ def tile_transformerblock_pa_t_kernel(tc, x, rms_w, w_qkv, out):
                 start=True,
                 stop=True,
             )
-            if t == 0:
-                y_tiles[c] = y_pool.tile([P, H, G, HD], F32, name="y")
-            copy(out=y_tiles[c][:, :, t, :], in_=acc[:])
-
-        def store(k, c):
-            nc.sync.dma_start(
-                out=out[c, k // GROUPS_PER_BATCH][:, rows_of(k), :].rearrange(
-                    "h (p t) j -> p h (t j)", t=G
-                ),
-                in_=y_tiles[c][:].rearrange("p h t j -> p h (t j)"),
-            )
+            if t == first:
+                y_tiles[c] = y_pool.tile([P, H, last - first, HD], F32, name="y")
+            copy(out=y_tiles[c][:, :, t - first, :], in_=acc[:])
+            if t == last - 1:
+                rows = out[c, b].rearrange("h (p t) j -> p h t j", t=T)[:, :, first:last, :]
+                nc.sync.dma_start(
+                    out=rows.rearrange("p h t j -> p h (t j)"),
+                    in_=y_tiles[c][:].rearrange("p h t j -> p h (t j)"),
+                )
 
         def measure(g):
             square_sum(g)
@@ -195,88 +191,99 @@ def tile_transformerblock_pa_t_kernel(tc, x, rms_w, w_qkv, out):
         make_identity(nc, ident[:])
         nc.scalar.dma_start(out=gain[:], in_=rms_w.rearrange("(q t) -> q t", t=PACK))
         stack.enter_context(tc.manual_schedule())
-        load_x(0, 2)
+        load_x(0, 0, 2)
+        load_x(0, 2, 4)
         load_w(0)
-        load_x(1, 1)
+        load_x(0, 4, T)
         load_w(1)
         load_w(2)
-        for k in range(2, GROUPS):
-            load_x(k, 1)
+        for b in range(1, B):
+            load_x(b, 0, T)
+
+        def copier(n):
+            return vector_copy if n % 2 == 1 and n % 24 != 23 else scalar_copy
 
         measure(0)
         scale(nc.vector, 0)
         scale(nc.vector, 1)
         flip_w(0)
+        flip(0)
+        flip(1)
         copy_w(vector_copy, 0, 0)
-        flip_two(0)
         measure(2)
-        copy_w(scalar_copy, 0, 1)
-        scale(nc.vector, 2)
-        scale(nc.vector, 3)
+        scale(nc.gpsimd, 2)
+        scale(nc.gpsimd, 3)
         pack(0)
         pack(1)
-        quantise_w(0)
+        flip(2)
+        flip(3)
+        square_sum(4)
+        copy_w(scalar_copy, 0, 1)
+        square_sum(5)
+        inverse_rms(4)
+        scale(nc.gpsimd, 4)
+        scale(nc.gpsimd, 5)
         quantise(0)
-        measure(G)
-        scale(nc.gpsimd, G)
-        scale(nc.gpsimd, G + 1)
-        flip_two(2)
+        quantise_w(0)
         pack(2)
         pack(3)
         flip_w(1)
-        copy_w(vector_copy, 1, 0)
-        copy_w(scalar_copy, 1, 1)
         quantise(2)
-        for t in range(G):
-            project(scalar_copy if t % 2 == 0 else vector_copy, 0, 0, t)
-        store(0, 0)
+        copy_w(scalar_copy, 1, 0)
+        copy_w(scalar_copy, 1, 1)
+        project(vector_copy, 0)
+        project(scalar_copy, 1)
         quantise_w(1)
         flip_w(2)
-        copy_w(vector_copy, 2, 0)
+        project(vector_copy, 2)
+        copy_w(scalar_copy, 2, 0)
+        project(scalar_copy, 3)
         copy_w(scalar_copy, 2, 1)
-        for t in range(G):
-            project(scalar_copy if t % 2 == 0 else vector_copy, 0, 1, t)
-        store(0, 1)
+        measure(6)
+        scale(nc.gpsimd, 6)
+        scale(nc.gpsimd, 7)
+        project(vector_copy, 4)
+        project(vector_copy, 5)
+        project(scalar_copy, 6)
         quantise_w(2)
-        measure(G + 2)
-        scale(nc.gpsimd, G + 2)
-        scale(nc.gpsimd, G + 3)
-        flip_two(G)
-        pack(G)
-        pack(G + 1)
-        for t in range(G):
-            project(scalar_copy if t % 2 == 0 else vector_copy, 0, 2, t)
-        store(0, 2)
-        quantise(G)
-        measure(2 * G)
-        scale(nc.gpsimd, 2 * G)
-        scale(nc.gpsimd, 2 * G + 1)
-        flip_two(G + 2)
-        pack(G + 2)
-        pack(G + 3)
-        quantise(G + 2)
+        project(vector_copy, 7)
+        flip(4)
+        flip(5)
+        pack(4)
+        pack(5)
+        quantise(4)
+        project(scalar_copy, 8)
+        project(scalar_copy, 9)
+        measure(8)
+        scale(nc.gpsimd, 8)
+        scale(nc.gpsimd, 9)
+        project(scalar_copy, 10)
+        flip(6)
+        flip(7)
+        pack(6)
+        pack(7)
+        quantise(6)
+        project(vector_copy, 11)
 
-        for i in range(2, 2 * GROUPS):
-            packed = 2 * (i + 2) if i + 2 < 2 * GROUPS else None
-            measured = 2 * (i + 3) if i + 3 < 2 * GROUPS else None
-            for m in range(6):
-                c, t = divmod(i % 2 * 6 + m, G)
-                if measured is not None:
-                    if m == 0:
-                        square_sum(measured)
-                        square_sum(measured + 1)
+        def step(first, last, packed, measured):
+            for n in range(first, last):
+                m = n - first
+                if measured < PAIRS:
                     if m == 2:
-                        inverse_rms(measured)
-                        scale(nc.gpsimd, measured)
-                        scale(nc.gpsimd, measured + 1)
-                if packed is not None:
+                        square_sum(2 * measured)
+                        square_sum(2 * measured + 1)
                     if m == 4:
-                        flip_two(packed)
-                        pack(packed)
-                    if m == 5:
-                        pack(packed + 1)
-                project(scalar_copy if m % 2 == 0 else vector_copy, i // 2, c, t)
-                if t == G - 1:
-                    store(i // 2, c)
-            if packed is not None:
-                quantise(packed)
+                        inverse_rms(2 * measured)
+                        scale(nc.gpsimd, 2 * measured)
+                        scale(nc.gpsimd, 2 * measured + 1)
+                if packed < PAIRS:
+                    if n == last - 2:
+                        flip_two(2 * packed)
+                        pack(2 * packed)
+                    if n == last - 1:
+                        pack(2 * packed + 1)
+                project(copier(n), n)
+            if packed < PAIRS:
+                quantise(2 * packed)
+        for i in range(2, PAIRS):
+            step(6 * i, 6 * i + 6, i + 2, i + 3)

@@ -77,10 +77,10 @@ def tile_transformerblock_pa_t_kernel(tc, x, rms_w, w_qkv, out):
                 out=sq[:], in_=tile_of(g), func=ACT.Square, accum_out=sumsq[:, g : g + 1]
             )
 
-        def inverse_rms(g):
+        def inverse_rms(g, count=2):
             nc.scalar.activation(
-                out=rinv[:, g : g + 2],
-                in_=sumsq[:, g : g + 2],
+                out=rinv[:, g : g + count],
+                in_=sumsq[:, g : g + count],
                 func=ACT.Abs_reciprocal_sqrt,
                 bias=eps[:],
                 scale=1.0 / D,
@@ -191,7 +191,8 @@ def tile_transformerblock_pa_t_kernel(tc, x, rms_w, w_qkv, out):
         make_identity(nc, ident[:])
         nc.scalar.dma_start(out=gain[:], in_=rms_w.rearrange("(q t) -> q t", t=PACK))
         stack.enter_context(tc.manual_schedule())
-        load_x(0, 0, 2)
+        load_x(0, 0, 1)
+        load_x(0, 1, 2)
         load_x(0, 2, 4)
         load_w(0)
         load_x(0, 4, T)
@@ -203,18 +204,24 @@ def tile_transformerblock_pa_t_kernel(tc, x, rms_w, w_qkv, out):
         def copier(n):
             return vector_copy if n % 2 == 1 and n % 24 != 23 else scalar_copy
 
-        measure(0)
+        square_sum(0)
+        inverse_rms(0, 1)
         scale(nc.vector, 0)
-        scale(nc.vector, 1)
-        flip_w(0)
         flip(0)
+        square_sum(1)
+        inverse_rms(1, 1)
+        scale(nc.vector, 1)
         flip(1)
-        copy_w(vector_copy, 0, 0)
-        measure(2)
+        square_sum(2)
+        inverse_rms(2, 1)
         scale(nc.gpsimd, 2)
+        square_sum(3)
+        inverse_rms(3, 1)
         scale(nc.gpsimd, 3)
         pack(0)
         pack(1)
+        flip_w(0)
+        copy_w(vector_copy, 0, 0)
         flip(2)
         flip(3)
         square_sum(4)
@@ -228,41 +235,43 @@ def tile_transformerblock_pa_t_kernel(tc, x, rms_w, w_qkv, out):
         pack(2)
         pack(3)
         flip_w(1)
-        quantise(2)
         copy_w(scalar_copy, 1, 0)
         copy_w(scalar_copy, 1, 1)
+        quantise(2)
         project(vector_copy, 0)
         project(scalar_copy, 1)
-        quantise_w(1)
         flip_w(2)
-        project(vector_copy, 2)
+        quantise_w(1)
         copy_w(scalar_copy, 2, 0)
-        project(scalar_copy, 3)
-        copy_w(scalar_copy, 2, 1)
         measure(6)
         scale(nc.gpsimd, 6)
         scale(nc.gpsimd, 7)
+        project(vector_copy, 2)
+        project(scalar_copy, 3)
+        copy_w(scalar_copy, 2, 1)
         project(vector_copy, 4)
         project(vector_copy, 5)
-        project(scalar_copy, 6)
-        quantise_w(2)
-        project(vector_copy, 7)
         flip(4)
         flip(5)
+        square_sum(8)
+        square_sum(9)
         pack(4)
+        quantise_w(2)
+        project(scalar_copy, 6)
+        project(vector_copy, 7)
         pack(5)
         quantise(4)
-        project(scalar_copy, 8)
-        project(scalar_copy, 9)
-        measure(8)
+        inverse_rms(8)
         scale(nc.gpsimd, 8)
         scale(nc.gpsimd, 9)
-        project(scalar_copy, 10)
+        project(scalar_copy, 8)
+        project(scalar_copy, 9)
         flip(6)
         flip(7)
         pack(6)
         pack(7)
         quantise(6)
+        project(scalar_copy, 10)
         project(vector_copy, 11)
 
         def step(first, last, packed, measured):

@@ -20,6 +20,7 @@ N = H * HD
 T = S // P
 PAIRS = B * T // 2
 GROUPS = [(b, i, i + 4) for b in range(B) for i in (0, 4)]
+WHOLE = [(b, 2) for b in range(1, B)]
 PRODUCTS = [(b, i, j, c, t) for b, i, j in GROUPS for c in range(C) for t in range(i, j)]
 
 FLOPS = 2 * B * S * C * N * D
@@ -34,6 +35,7 @@ def tile_transformerblock_pa_t_kernel(tc, x, rms_w, w_qkv, out):
         grouped_pool = stack.enter_context(tc.tile_pool(name="grouped", bufs=4))
         w_grouped_pool = stack.enter_context(tc.tile_pool(name="w_grouped", bufs=2))
         y_pool = stack.enter_context(tc.tile_pool(name="y", bufs=7))
+        whole_pool = stack.enter_context(tc.tile_pool(name="y_whole", bufs=3))
         flip_pool = stack.enter_context(tc.psum_pool(name="flip", bufs=2))
         acc_pool = stack.enter_context(tc.psum_pool(name="acc", bufs=6))
 
@@ -63,8 +65,8 @@ def tile_transformerblock_pa_t_kernel(tc, x, rms_w, w_qkv, out):
 
         def load_w(c):
             nc.sync.dma_start(
-                out=w_sb[c][:].rearrange("p (i k) -> p i k", k=D),
-                in_=w_qkv[c * N : (c + 1) * N, :].rearrange("(i p) k -> p i k", p=P),
+                out=w_sb[c][:],
+                in_=w_qkv[c * N : (c + 1) * N, :].rearrange("(p i) k -> p (i k)", p=P),
             )
 
         def tile_of(g):
@@ -155,9 +157,9 @@ def tile_transformerblock_pa_t_kernel(tc, x, rms_w, w_qkv, out):
             b, first, last, c, t = PRODUCTS[n]
             tok = slice((b * T + t) * P, (b * T + t + 1) * P)
             feat = slice(c * N, (c + 1) * N)
-            acc = acc_pool.tile([P, H, HD], F32, name="acc")
+            acc = acc_pool.tile([P, N], F32, name="acc")
             nc.tensor.matmul_mx(
-                out=acc[:].rearrange("p h j -> p (h j)"),
+                out=acc[:],
                 lhsT=x_codes[:, tok].bitcast(FP8X4),
                 lhsT_scale=x_scales[:, tok],
                 rhs=w_codes[:, feat].bitcast(FP8X4),
@@ -165,9 +167,17 @@ def tile_transformerblock_pa_t_kernel(tc, x, rms_w, w_qkv, out):
                 start=True,
                 stop=True,
             )
+            whole = (b, c) in WHOLE
+            if whole:
+                first, last = 0, T
             if t == first:
-                y_tiles[c] = y_pool.tile([P, H, last - first, HD], F32, name="y")
-            copy(out=y_tiles[c][:, :, t - first, :], in_=acc[:])
+                name = "y_whole" if whole else "y"
+                pool = whole_pool if whole else y_pool
+                y_tiles[c] = pool.tile([P, H, last - first, HD], F32, name=name)
+            copy(
+                out=y_tiles[c][:, :, t - first, :].rearrange("p h (q i) -> p h q i", i=4),
+                in_=acc[:].rearrange("p (i h q) -> p h q i", i=4, h=H),
+            )
             if t == last - 1:
                 rows = out[c, b].rearrange("h (p t) j -> p h t j", t=T)[:, :, first:last, :]
                 nc.sync.dma_start(

from contextlib import ExitStack

import concourse.mybir as mybir
from concourse.masks import make_identity

F32 = mybir.dt.float32
BF16 = mybir.dt.bfloat16
U32 = mybir.dt.uint32
U8 = mybir.dt.uint8
FP8X4 = mybir.dt.float8_e4m3fn_x4
ACT = mybir.ActivationFunctionType
ALU = mybir.AluOpType

P = 128
PACK = 4
B, S, D = 4, 1024, 512
C, H, HD = 3, 4, 128
EPS = 1e-5
N = H * HD
T = S // P
PAIRS = B * T // 2
GROUPS = [(b, i, i + 4) for b in range(B) for i in (0, 4)]
WHOLE = [(b, 2) for b in range(1, B)]
PRODUCTS = [(b, i, j, c, t) for b, i, j in GROUPS for c in range(C) for t in range(i, j)]

FLOPS = 2 * B * S * C * N * D


def tile_transformerblock_pa_t_kernel(tc, x, rms_w, w_qkv, out):
    nc = tc.nc
    with ExitStack() as stack:
        keep = stack.enter_context(tc.tile_pool(name="keep", bufs=1))
        squares = stack.enter_context(tc.tile_pool(name="squares", bufs=2))
        scaled_pool = stack.enter_context(tc.tile_pool(name="scaled", bufs=8))
        grouped_pool = stack.enter_context(tc.tile_pool(name="grouped", bufs=4))
        w_grouped_pool = stack.enter_context(tc.tile_pool(name="w_grouped", bufs=2))
        y_pool = stack.enter_context(tc.tile_pool(name="y", bufs=7))
        whole_pool = stack.enter_context(tc.tile_pool(name="y_whole", bufs=3))
        flip_pool = stack.enter_context(tc.psum_pool(name="flip", bufs=2))
        acc_pool = stack.enter_context(tc.psum_pool(name="acc", bufs=6))

        ident = keep.tile([P, P], F32, name="ident")
        eps = keep.tile([P, 1], F32, name="eps")
        warm = keep.tile([P, 1], F32, name="warm")
        gain = keep.tile([P, PACK], BF16, name="gain")
        sumsq = keep.tile([P, B * T], F32, name="sumsq")
        rinv = keep.tile([P, B * T], F32, name="rinv")
        x_sb = [keep.tile([P, T * D], BF16, name="x%d" % b) for b in range(B)]
        w_sb = [keep.tile([P, PACK * D], BF16, name="w%d" % c) for c in range(C)]
        x_codes = keep.tile([P, B * T * P], U32, name="x_codes", align_bytes=64)
        x_scales = keep.tile([P, B * T * P], U8, name="x_scales", align_bytes=64)
        w_codes = keep.tile([P, C * N], U32, name="w_codes", align_bytes=64)
        w_scales = keep.tile([P, C * N], U8, name="w_scales", align_bytes=64)
        scaled = {}
        flipped = {}
        grouped = {}
        w_flipped = {}
        w_grouped = {}
        y_tiles = {}

        def load_x(b, first, last):
            cols = slice(first * D, last * D)
            rows = x[b].rearrange("(p t) d -> p (t d)", t=T)
            nc.sync.dma_start(out=x_sb[b][:, cols], in_=rows[:, cols])

        def load_w(c):
            nc.sync.dma_start(
                out=w_sb[c][:],
                in_=w_qkv[c * N : (c + 1) * N, :].rearrange("(p i) k -> p (i k)", p=P),
            )

        def tile_of(g):
            b, t = divmod(g, T)
            return x_sb[b][:, t * D : (t + 1) * D]

        def square_sum(g):
            sq = squares.tile([P, D], BF16, name="sq")
            nc.scalar.activation(
                out=sq[:], in_=tile_of(g), func=ACT.Square, accum_out=sumsq[:, g : g + 1]
            )

        def inverse_rms(g, count=2):
            nc.scalar.activation(
                out=rinv[:, g : g + count],
                in_=sumsq[:, g : g + count],
                func=ACT.Abs_reciprocal_sqrt,
                bias=eps[:],
                scale=1.0 / D,
            )

        def scale(engine, g):
            scaled[g] = scaled_pool.tile([P, PACK, P], F32, name="scaled")
            engine.tensor_scalar(
                out=scaled[g][:],
                in0=tile_of(g).rearrange("p (q t) -> p t q", t=PACK),
                scalar1=rinv[:, g : g + 1],
                scalar2=1.0,
                op0=ALU.mult,
                op1=ALU.mult,
            )

        def flip(g):
            flipped[g] = flip_pool.tile([P, PACK, P], F32, name="flipped")
            for t in range(PACK):
                nc.tensor.transpose(flipped[g][:, t, :], scaled[g][:, t, :], ident[:])

        def pack(g):
            if g % 2 == 0:
                grouped[g // 2] = grouped_pool.tile(
                    [P, 2 * P * PACK], BF16, name="grouped", align_bytes=64
                )
            k = g % 2
            nc.vector.tensor_tensor(
                out=grouped[g // 2][:, k * P * PACK : (k + 1) * P * PACK].rearrange(
                    "p (r t) -> p r t", t=PACK
                ),
                in0=flipped[g][:].rearrange("p t r -> p r t"),
                in1=gain[:].unsqueeze(1).to_broadcast([P, P, PACK]),
                op=ALU.mult,
            )

        def quantise(g):
            cols = slice(g * P, (g + 2) * P)
            nc.vector.quantize_mx(
                out=x_codes[:, cols].bitcast(FP8X4),
                scales=x_scales[:, cols],
                in_=grouped[g // 2][:],
            )

        def flip_w(c):
            w_words = w_sb[c][:].bitcast(F32)
            for k in range(2):
                w_flipped[(c, k)] = acc_pool.tile([P, PACK, P], F32, name="acc")
                for s in range(PACK):
                    i, u = divmod(k * PACK + s, 2)
                    words = w_words[:, i * D // 2 + u : (i + 1) * D // 2 : 2]
                    nc.tensor.transpose(w_flipped[(c, k)][:, s, :], words, ident[:])

        def copy_w(copy, c, k):
            if k == 0:
                w_grouped[c] = w_grouped_pool.tile(
                    [P, N * PACK], BF16, name="w_grouped", align_bytes=64
                )
            words = w_grouped[c][:].bitcast(F32)[:, k * N : (k + 1) * N]
            copy(
                out=words.rearrange("p (i f u) -> p i f u", i=2, u=2),
                in_=w_flipped[(c, k)][:].rearrange("p (i u) f -> p i f u", u=2),
            )

        def quantise_w(c):
            cols = slice(c * N, (c + 1) * N)
            nc.vector.quantize_mx(
                out=w_codes[:, cols].bitcast(FP8X4), scales=w_scales[:, cols], in_=w_grouped[c][:]
            )

        def project(copy, n):
            b, first, last, c, t = PRODUCTS[n]
            tok = slice((b * T + t) * P, (b * T + t + 1) * P)
            feat = slice(c * N, (c + 1) * N)
            acc = acc_pool.tile([P, N], F32, name="acc")
            nc.tensor.matmul_mx(
                out=acc[:],
                lhsT=x_codes[:, tok].bitcast(FP8X4),
                lhsT_scale=x_scales[:, tok],
                rhs=w_codes[:, feat].bitcast(FP8X4),
                rhs_scale=w_scales[:, feat],
                start=True,
                stop=True,
            )
            whole = (b, c) in WHOLE
            if whole:
                first, last = 0, T
            if t == first:
                name = "y_whole" if whole else "y"
                pool = whole_pool if whole else y_pool
                y_tiles[c] = pool.tile([P, H, last - first, HD], F32, name=name)
            copy(
                out=y_tiles[c][:, :, t - first, :].rearrange("p h (q i) -> p h q i", i=4),
                in_=acc[:].rearrange("p (i h q) -> p h q i", i=4, h=H),
            )
            if t == last - 1:
                rows = out[c, b].rearrange("h (p t) j -> p h t j", t=T)[:, :, first:last, :]
                nc.sync.dma_start(
                    out=rows.rearrange("p h t j -> p h (t j)"),
                    in_=y_tiles[c][:].rearrange("p h t j -> p h (t j)"),
                )

        def measure(g):
            square_sum(g)
            square_sum(g + 1)
            inverse_rms(g)

        def flip_two(g):
            flip(g)
            flip(g + 1)

        scalar_copy, vector_copy = nc.scalar.copy, nc.vector.tensor_copy

        nc.vector.memset(eps[:], EPS)
        nc.scalar.activation(out=warm[:], in_=eps[:], func=ACT.Abs_reciprocal_sqrt)
        make_identity(nc, ident[:])
        nc.scalar.dma_start(out=gain[:], in_=rms_w.rearrange("(q t) -> q t", t=PACK))
        stack.enter_context(tc.manual_schedule())
        load_x(0, 0, 1)
        load_x(0, 1, 2)
        load_x(0, 2, 4)
        load_w(0)
        load_x(0, 4, T)
        load_w(1)
        load_w(2)
        for b in range(1, B):
            load_x(b, 0, T)

        def copier(n):
            return vector_copy if n % 2 == 1 and n % 24 != 23 else scalar_copy

        square_sum(0)
        inverse_rms(0, 1)
        scale(nc.vector, 0)
        flip(0)
        square_sum(1)
        inverse_rms(1, 1)
        scale(nc.vector, 1)
        flip(1)
        square_sum(2)
        inverse_rms(2, 1)
        scale(nc.gpsimd, 2)
        square_sum(3)
        inverse_rms(3, 1)
        scale(nc.gpsimd, 3)
        pack(0)
        pack(1)
        flip_w(0)
        copy_w(vector_copy, 0, 0)
        flip(2)
        flip(3)
        square_sum(4)
        copy_w(scalar_copy, 0, 1)
        square_sum(5)
        inverse_rms(4)
        scale(nc.gpsimd, 4)
        scale(nc.gpsimd, 5)
        quantise(0)
        quantise_w(0)
        pack(2)
        pack(3)
        flip_w(1)
        copy_w(scalar_copy, 1, 0)
        copy_w(scalar_copy, 1, 1)
        quantise(2)
        project(vector_copy, 0)
        project(scalar_copy, 1)
        flip_w(2)
        quantise_w(1)
        copy_w(scalar_copy, 2, 0)
        measure(6)
        scale(nc.gpsimd, 6)
        scale(nc.gpsimd, 7)
        project(vector_copy, 2)
        project(scalar_copy, 3)
        copy_w(scalar_copy, 2, 1)
        project(vector_copy, 4)
        project(vector_copy, 5)
        flip(4)
        flip(5)
        square_sum(8)
        square_sum(9)
        pack(4)
        quantise_w(2)
        project(scalar_copy, 6)
        project(vector_copy, 7)
        pack(5)
        quantise(4)
        inverse_rms(8)
        scale(nc.gpsimd, 8)
        scale(nc.gpsimd, 9)
        project(scalar_copy, 8)
        project(scalar_copy, 9)
        flip(6)
        flip(7)
        pack(6)
        pack(7)
        quantise(6)
        project(scalar_copy, 10)
        project(vector_copy, 11)

        def step(first, last, packed, measured):
            for n in range(first, last):
                m = n - first
                if measured < PAIRS:
                    if m == 2:
                        square_sum(2 * measured)
                        square_sum(2 * measured + 1)
                    if m == 4:
                        inverse_rms(2 * measured)
                        scale(nc.gpsimd, 2 * measured)
                        scale(nc.gpsimd, 2 * measured + 1)
                if packed < PAIRS:
                    if n == last - 2:
                        flip_two(2 * packed)
                        pack(2 * packed)
                    if n == last - 1:
                        pack(2 * packed + 1)
                project(copier(n), n)
            if packed < PAIRS:
                quantise(2 * packed)
        for i in range(2, PAIRS):
            step(6 * i, 6 * i + 6, i + 2, i + 3)
